import numpy as np
import ml_dtypes


def mxq(x, axis, fmt="e4m3"):
    dtype, down = {"e4m3": (ml_dtypes.float8_e4m3fn, 7), "e5m2": (ml_dtypes.float8_e5m2, 14)}[fmt]
    v = np.moveaxis(np.asarray(x, np.float32).astype(ml_dtypes.bfloat16).astype(np.float64), axis, -1)
    blocks = v.reshape(v.shape[:-1] + (-1, 32))
    amax = np.abs(blocks).max(-1, keepdims=True)
    byte = np.maximum(np.where(amax > 0, np.frexp(amax)[1] - 1 + 127, 0) - down, 1)
    scale = np.exp2(byte - 127.0)
    codes = (blocks / scale).astype(np.float32).astype(dtype).astype(np.float64)
    return np.moveaxis((codes * scale).reshape(v.shape), -1, axis)


WIDE = False


def mx_kscale(k):
    if not WIDE:
        return np.ones(k)
    levels = np.array([20, -20, 10, -10, 0])
    a = np.random.permutation(np.resize(levels, k // 512 * 4)).reshape(k // 512, 4)
    idx = np.arange(k)
    return np.exp2(a[idx // 512, idx % 128 // 32])


BF16 = ml_dtypes.bfloat16


def bf(x):
    return np.asarray(x, np.float32).astype(BF16)


def f64(x):
    return np.asarray(x).astype(np.float64)


B, N, I, O = 256, 4, 128, 8192
WS = 0.7 / np.sqrt(I)
GS = 16.0


def setup_inputs():
    u = mx_kscale(O)
    x = np.random.standard_normal((B, N, I)).reshape(B, N * I)
    w_self = np.random.standard_normal((N, O, I)) * WS / u[:, None]
    w_parent = np.random.standard_normal((N - 1, O, I)) * WS / u[:, None]
    bias = np.random.standard_normal(N * O) * 0.5
    g = np.random.standard_normal((B, N, O)) * np.exp2(np.random.randint(-12, 1, (B, 1, 1))) * GS * u
    return {"x": bf(x), "w_self": bf(w_self), "w_parent": bf(w_parent), "bias": bf(bias),
            "grad_out": bf(g.reshape(B, N * O))}


def reference(x, w_self, w_parent, bias, grad_out):
    gq = mxq(f64(grad_out).reshape(B, N, O).transpose(1, 0, 2), 2, "e5m2")
    d_self = gq @ mxq(f64(w_self), 1, "e4m3")
    d_par = gq[1:] @ mxq(f64(w_parent), 1, "e4m3")
    d = np.concatenate([d_self[:-1] + d_par, d_self[-1:]], 0)
    return d.transpose(1, 0, 2).reshape(B, N * I)

@@ -1,0 +1,185 @@
+from contextlib import ExitStack
+
+import concourse.mybir as mybir
+from concourse.masks import make_identity
+
+F32 = mybir.dt.float32
+BF16 = mybir.dt.bfloat16
+I32 = mybir.dt.int32
+U32 = mybir.dt.uint32
+U8 = mybir.dt.uint8
+E4M3_X4 = mybir.dt.float8_e4m3fn_x4
+E5M2_X4 = mybir.dt.float8_e5m2_x4
+
+P = 128
+PACK = 4
+K_PASS = P * PACK
+PAIR = 2
+
+BATCH = 256
+HALVES = BATCH // P
+JOINTS = 4
+IN_CH = 128
+OUT_CH = 8192
+MOVING = 512
+
+ROUND_PASSES = 4
+ROUND_K = ROUND_PASSES * K_PASS
+ROUNDS_PER_JOINT = OUT_CH // ROUND_K
+ROUNDS = JOINTS * ROUNDS_PER_JOINT
+ROUND_COLS = ROUND_PASSES * BATCH
+PAD_COLS = MOVING - BATCH
+EDGES = 2
+
+RAW_BUFS = 4
+CODE_BUFS = 3
+
+FLOPS = 2 * BATCH * OUT_CH * IN_CH * (2 * JOINTS - 1)
+
+
+def tile_skeletonlinear_pa_k_kernel(tc, x, w_self, w_parent, bias, grad_out, out):
+    nc = tc.nc
+    g_rows = grad_out.rearrange("(h b) k -> b h k", h=HALVES)
+    out_rows = out.rearrange("(h b) c -> b h c", h=HALVES)
+
+    def edges_of(joint):
+        edges = [(w_self[joint], joint)]
+        if joint > 0:
+            edges.append((w_parent[joint - 1], joint - 1))
+        return edges
+
+    with ExitStack() as ctx:
+        ctx.enter_context(tc.manual_schedule())
+        keep = ctx.enter_context(tc.tile_pool(name="keep", bufs=1))
+        raw = ctx.enter_context(tc.tile_pool(name="raw", bufs=RAW_BUFS))
+        grouped = ctx.enter_context(tc.tile_pool(name="grouped", bufs=2))
+        codes = ctx.enter_context(tc.tile_pool(name="codes", bufs=CODE_BUFS))
+        sums = ctx.enter_context(tc.psum_pool(name="sums", bufs=1))
+        banks = ctx.enter_context(tc.psum_pool(name="banks", bufs=4))
+
+        g_raw = {}
+        w_raw = {}
+
+        def load(r):
+            joint, part = divmod(r, ROUNDS_PER_JOINT)
+            k0 = part * ROUND_K
+            g_raw[r] = raw.tile([P, HALVES, ROUND_K], BF16, name="g_raw")
+            col0 = joint * OUT_CH + k0
+            nc.sync.dma_start(out=g_raw[r][:], in_=g_rows[:, :, col0 : col0 + ROUND_K])
+            for e, (weight, target) in enumerate(edges_of(joint)):
+                w_raw[r, e] = raw.tile([P, ROUND_PASSES, PACK, IN_CH], BF16, name="w_raw%d" % e)
+                nc.sync.dma_start(
+                    out=w_raw[r, e][:],
+                    in_=weight[k0 : k0 + ROUND_K, :].rearrange("(c p t) i -> p c t i", p=P, t=PACK),
+                )
+
+        for r in range(RAW_BUFS):
+            load(r)
+
+        identity = keep.tile([P, P], F32, name="identity")
+        make_identity(nc, identity[:])
+
+        g_codes = []
+        g_scales = []
+        for i in range(CODE_BUFS):
+            g_codes.append(keep.tile([P, ROUND_COLS + PAD_COLS], U32, name="g_codes%d" % i, align_bytes=64))
+            g_scales.append(keep.tile([P, ROUND_COLS + PAD_COLS], U8, name="g_scales%d" % i, align_bytes=64))
+            nc.vector.memset(g_codes[i][:, ROUND_COLS:].bitcast(I32), 0)
+            nc.vector.memset(g_scales[i][:, ROUND_COLS:].bitcast(I32), 0)
+
+        acc = [sums.tile([P, MOVING], F32, name="acc%d" % j) for j in range(JOINTS)]
+
+        w_codes = {}
+        w_scales = {}
+
+        def prepare(r):
+            joint = r // ROUNDS_PER_JOINT
+            edges = edges_of(joint)
+
+            g_grouped = grouped.tile([P, ROUND_COLS * PACK], BF16, name="g_grouped", align_bytes=64)
+            g_grouped_words = g_grouped[:].bitcast(F32)
+            for c in range(ROUND_PASSES):
+                bank = banks.tile([P, HALVES, PAIR, P], F32, name="bank")
+                word0 = c * K_PASS // PAIR
+                for h in range(HALVES):
+                    g_words = g_raw[r][:, h, :].bitcast(F32)
+                    for u in range(PAIR):
+                        nc.tensor.transpose(
+                            bank[:, h, u, :],
+                            g_words[:, word0 + u : word0 + K_PASS // PAIR : PAIR],
+                            identity[:],
+                        )
+                nc.scalar.copy(
+                    out=g_grouped_words[:, c * BATCH * PAIR : (c + 1) * BATCH * PAIR].rearrange(
+                        "p (h b u) -> p h b u", h=HALVES, u=PAIR
+                    ),
+                    in_=bank[:].rearrange("p h u b -> p h b u"),
+                )
+
+            w_grouped = grouped.tile([P, EDGES, ROUND_PASSES, IN_CH, PACK], BF16, name="w_grouped", align_bytes=64)
+            for e in range(len(edges)):
+                if e == 0:
+                    nc.vector.tensor_copy(
+                        out=w_grouped[:, e].rearrange("p c (g i) t -> p c g t i", i=PACK),
+                        in_=w_raw[r, e][:].rearrange("p c t (g i) -> p c g t i", i=PACK),
+                    )
+                else:
+                    for c in range(ROUND_PASSES):
+                        nc.scalar.copy(
+                            out=w_grouped[:, e, c].rearrange("p (g i) t -> p g t i", i=PACK),
+                            in_=w_raw[r, e][:, c].rearrange("p t (g i) -> p g t i", i=PACK),
+                        )
+
+            slot = r % CODE_BUFS
+            nc.vector.quantize_mx(
+                out=g_codes[slot][:, :ROUND_COLS].bitcast(E5M2_X4),
+                scales=g_scales[slot][:, :ROUND_COLS],
+                in_=g_grouped[:],
+            )
+            w_codes[r] = codes.tile([P, EDGES, ROUND_PASSES, IN_CH], U32, name="w_codes", align_bytes=64)
+            w_scales[r] = codes.tile([P, EDGES, ROUND_PASSES, IN_CH], U8, name="w_scales", align_bytes=64)
+            for e in range(len(edges)):
+                nc.vector.quantize_mx(
+                    out=w_codes[r][:, e].rearrange("p c i -> p (c i)").bitcast(E4M3_X4),
+                    scales=w_scales[r][:, e].rearrange("p c i -> p (c i)"),
+                    in_=w_grouped[:, e].rearrange("p c i t -> p (c i t)"),
+                )
+
+        def multiply(r):
+            joint, part = divmod(r, ROUNDS_PER_JOINT)
+            slot = r % CODE_BUFS
+            for e, (weight, target) in enumerate(edges_of(joint)):
+                opens = e == 0 and part == 0
+                closes = part == ROUNDS_PER_JOINT - 1 and (e == 1 or joint == JOINTS - 1)
+                for c in range(ROUND_PASSES):
+                    nc.tensor.matmul_mx(
+                        out=acc[target][:],
+                        lhsT=w_codes[r][:, e, c, :].bitcast(E4M3_X4),
+                        lhsT_scale=w_scales[r][:, e, c, :],
+                        rhs=g_codes[slot][:, c * BATCH : c * BATCH + MOVING].bitcast(E5M2_X4),
+                        rhs_scale=g_scales[slot][:, c * BATCH : c * BATCH + MOVING],
+                        start=(opens and c == 0),
+                        stop=(closes and c == ROUND_PASSES - 1),
+                    )
+
+        for r in range(ROUNDS + 1):
+            if r < ROUNDS:
+                prepare(r)
+            if r + RAW_BUFS < ROUNDS:
+                load(r + RAW_BUFS)
+            if r > 0:
+                multiply(r - 1)
+
+        copy_of = [nc.vector.tensor_copy if j % 2 == 0 else nc.scalar.copy for j in range(JOINTS)]
+        sum_t = [keep.tile([P, BATCH], F32, name="sum_t%d" % j) for j in range(JOINTS)]
+        out_sb = keep.tile([P, HALVES, JOINTS, IN_CH], F32, name="out_sb")
+        for j in range(JOINTS):
+            copy_of[j](out=sum_t[j][:], in_=acc[j][:, :BATCH])
+        turned = []
+        for j in range(JOINTS):
+            turned.append(banks.tile([P, HALVES, PAIR, P], F32, name="bank"))
+            for h in range(HALVES):
+                nc.tensor.transpose(turned[j][:, h, 0, :], sum_t[j][:, h * P : (h + 1) * P], identity[:])
+        for j in range(JOINTS):
+            copy_of[j](out=out_sb[:, :, j, :], in_=turned[j][:, :, 0, :])
+            nc.sync.dma_start(out=out_rows[:, :, j * IN_CH : (j + 1) * IN_CH], in_=out_sb[:, :, j, :])

@@ -21,18 +21,22 @@ HALVES = BATCH // P
 JOINTS = 4
 IN_CH = 128
 OUT_CH = 8192
-MOVING = 512
+PASSES = OUT_CH // K_PASS
+OUT_COLS = JOINTS * IN_CH
 
-ROUND_PASSES = 4
-ROUND_K = ROUND_PASSES * K_PASS
-ROUNDS_PER_JOINT = OUT_CH // ROUND_K
-ROUNDS = JOINTS * ROUNDS_PER_JOINT
-ROUND_COLS = ROUND_PASSES * BATCH
-PAD_COLS = MOVING - BATCH
-EDGES = 2
+UNIT = 4
+LAST_UNITS = [4, 4, 4, 2, 1, 1]
+FIRST_PIECES = [1, 1, 2]
 
-RAW_BUFS = 4
-CODE_BUFS = 3
+EDGE_COLS = 2 * IN_CH
+GAP = OUT_COLS - EDGE_COLS
+PASS_COLS = EDGE_COLS + GAP
+W_COLS = UNIT * PASS_COLS + GAP
+G_COLS = UNIT * BATCH
+PAD_COLS = OUT_COLS - BATCH
+
+RAW_BUFS = 5
+SLOTS = 4
 
 FLOPS = 2 * BATCH * OUT_CH * IN_CH * (2 * JOINTS - 1)
 
@@ -40,69 +44,97 @@ FLOPS = 2 * BATCH * OUT_CH * IN_CH * (2 * JOINTS - 1)
 def tile_skeletonlinear_pa_k_kernel(tc, x, w_self, w_parent, bias, grad_out, out):
     nc = tc.nc
     g_rows = grad_out.rearrange("(h b) k -> b h k", h=HALVES)
-    out_rows = out.rearrange("(h b) c -> b h c", h=HALVES)
 
     def edges_of(joint):
-        edges = [(w_self[joint], joint)]
-        if joint > 0:
-            edges.append((w_parent[joint - 1], joint - 1))
-        return edges
+        return [w_parent[joint - 1], w_self[joint]] if joint > 0 else [w_self[joint]]
+
+    units = []
+    for joint in range(JOINTS):
+        pass0 = 0
+        for passes in LAST_UNITS if joint == JOINTS - 1 else [UNIT] * (PASSES // UNIT):
+            units.append((joint, pass0, passes))
+            pass0 += passes
+    count = len(units)
 
     with ExitStack() as ctx:
         ctx.enter_context(tc.manual_schedule())
         keep = ctx.enter_context(tc.tile_pool(name="keep", bufs=1))
         raw = ctx.enter_context(tc.tile_pool(name="raw", bufs=RAW_BUFS))
         grouped = ctx.enter_context(tc.tile_pool(name="grouped", bufs=2))
-        codes = ctx.enter_context(tc.tile_pool(name="codes", bufs=CODE_BUFS))
         sums = ctx.enter_context(tc.psum_pool(name="sums", bufs=1))
-        banks = ctx.enter_context(tc.psum_pool(name="banks", bufs=4))
+        banks = ctx.enter_context(tc.psum_pool(name="banks", bufs=5))
 
         g_raw = {}
         w_raw = {}
 
-        def load(r):
-            joint, part = divmod(r, ROUNDS_PER_JOINT)
-            k0 = part * ROUND_K
-            g_raw[r] = raw.tile([P, HALVES, ROUND_K], BF16, name="g_raw")
-            col0 = joint * OUT_CH + k0
-            nc.sync.dma_start(out=g_raw[r][:], in_=g_rows[:, :, col0 : col0 + ROUND_K])
-            for e, (weight, target) in enumerate(edges_of(joint)):
-                w_raw[r, e] = raw.tile([P, ROUND_PASSES, PACK, IN_CH], BF16, name="w_raw%d" % e)
+        def load_g(i):
+            if i >= count:
+                return
+            joint, pass0, passes = units[i]
+            col0 = joint * OUT_CH + pass0 * K_PASS
+            g_raw[i] = raw.tile([P, HALVES, passes * K_PASS], BF16, name="g_raw")
+            k0 = 0
+            for n in FIRST_PIECES if i == 0 else [passes]:
+                k1 = k0 + n * K_PASS
+                nc.sync.dma_start(out=g_raw[i][:, :, k0:k1], in_=g_rows[:, :, col0 + k0 : col0 + k1])
+                k0 = k1
+
+        def load_w(i):
+            if i >= count:
+                return
+            joint, pass0, passes = units[i]
+            rows = slice(pass0 * K_PASS, (pass0 + passes) * K_PASS)
+            for e, weight in enumerate(edges_of(joint)):
+                w_raw[i, e] = raw.tile([P, passes, PACK, IN_CH], BF16, name="w_raw%d" % e)
                 nc.sync.dma_start(
-                    out=w_raw[r, e][:],
-                    in_=weight[k0 : k0 + ROUND_K, :].rearrange("(c p t) i -> p c t i", p=P, t=PACK),
+                    out=w_raw[i, e][:], in_=weight[rows, :].rearrange("(c p t) i -> p c t i", p=P, t=PACK)
                 )
 
-        for r in range(RAW_BUFS):
-            load(r)
+        load_g(0)
+        for i in range(1, RAW_BUFS):
+            load_g(i)
+            load_w(i - 1)
+        load_w(RAW_BUFS - 1)
 
         identity = keep.tile([P, P], F32, name="identity")
         make_identity(nc, identity[:])
 
+        w_codes = []
+        w_scales = []
         g_codes = []
         g_scales = []
-        for i in range(CODE_BUFS):
-            g_codes.append(keep.tile([P, ROUND_COLS + PAD_COLS], U32, name="g_codes%d" % i, align_bytes=64))
-            g_scales.append(keep.tile([P, ROUND_COLS + PAD_COLS], U8, name="g_scales%d" % i, align_bytes=64))
-            nc.vector.memset(g_codes[i][:, ROUND_COLS:].bitcast(I32), 0)
-            nc.vector.memset(g_scales[i][:, ROUND_COLS:].bitcast(I32), 0)
+        for i in range(SLOTS):
+            w_codes.append(keep.tile([P, W_COLS], U32, name="w_codes%d" % i, align_bytes=64))
+            w_scales.append(keep.tile([P, W_COLS], U8, name="w_scales%d" % i, align_bytes=64))
+            g_codes.append(keep.tile([P, G_COLS + PAD_COLS], U32, name="g_codes%d" % i, align_bytes=64))
+            g_scales.append(keep.tile([P, G_COLS + PAD_COLS], U8, name="g_scales%d" % i, align_bytes=64))
+            nc.gpsimd.memset(g_codes[i][:, G_COLS:].bitcast(I32), 0)
+            nc.gpsimd.memset(g_scales[i][:, G_COLS:].bitcast(I32), 0)
+            engine = nc.vector if i < SLOTS // 2 else nc.gpsimd
+            for plane in (w_codes[i][:], w_scales[i][:]):
+                words = plane.bitcast(I32)
+                blocks = words.rearrange("p (n w) -> p n w", n=W_COLS // GAP)
+                engine.memset(blocks[:, 0 : W_COLS // GAP : 2, :], 0)
 
-        acc = [sums.tile([P, MOVING], F32, name="acc%d" % j) for j in range(JOINTS)]
+        acc = [sums.tile([P, OUT_COLS], F32, name="acc%d" % h) for h in range(HALVES)]
+        acc_t = sums.tile([P, OUT_COLS], F32, name="acc_t")
+        sum_t = keep.tile([P, BATCH], F32, name="sum_t")
+        first = keep.tile([P, HALVES, IN_CH], F32, name="first")
 
-        w_codes = {}
-        w_scales = {}
+        g_grouped = {}
+        w_grouped = {}
 
-        def prepare(r):
-            joint = r // ROUNDS_PER_JOINT
-            edges = edges_of(joint)
-
-            g_grouped = grouped.tile([P, ROUND_COLS * PACK], BF16, name="g_grouped", align_bytes=64)
-            g_grouped_words = g_grouped[:].bitcast(F32)
-            for c in range(ROUND_PASSES):
+        def transpose_g(i):
+            if i >= count:
+                return
+            passes = units[i][2]
+            g_grouped[i] = grouped.tile([P, passes * BATCH * PACK], BF16, name="g_grouped", align_bytes=64)
+            g_grouped_words = g_grouped[i][:].bitcast(F32)
+            for c in range(passes):
                 bank = banks.tile([P, HALVES, PAIR, P], F32, name="bank")
                 word0 = c * K_PASS // PAIR
                 for h in range(HALVES):
-                    g_words = g_raw[r][:, h, :].bitcast(F32)
+                    g_words = g_raw[i][:, h, :].bitcast(F32)
                     for u in range(PAIR):
                         nc.tensor.transpose(
                             bank[:, h, u, :],
@@ -116,70 +148,106 @@ def tile_skeletonlinear_pa_k_kernel(tc, x, w_self, w_parent, bias, grad_out, out
                     in_=bank[:].rearrange("p h u b -> p h b u"),
                 )
 
-            w_grouped = grouped.tile([P, EDGES, ROUND_PASSES, IN_CH, PACK], BF16, name="w_grouped", align_bytes=64)
-            for e in range(len(edges)):
-                if e == 0:
+        def group_w(i):
+            joint, pass0, passes = units[i]
+            edges = len(edges_of(joint))
+            w_grouped[i] = grouped.tile([P, passes, edges, IN_CH, PACK], BF16, name="w_grouped", align_bytes=64)
+            for e in range(edges):
+                if e == edges - 1:
                     nc.vector.tensor_copy(
-                        out=w_grouped[:, e].rearrange("p c (g i) t -> p c g t i", i=PACK),
-                        in_=w_raw[r, e][:].rearrange("p c t (g i) -> p c g t i", i=PACK),
+                        out=w_grouped[i][:, :, e].rearrange("p c (g i) t -> p c g t i", i=PACK),
+                        in_=w_raw[i, e][:].rearrange("p c t (g i) -> p c g t i", i=PACK),
                     )
                 else:
-                    for c in range(ROUND_PASSES):
-                        nc.scalar.copy(
-                            out=w_grouped[:, e, c].rearrange("p (g i) t -> p g t i", i=PACK),
-                            in_=w_raw[r, e][:, c].rearrange("p t (g i) -> p g t i", i=PACK),
+                    for c in range(passes):
+                        copy = nc.vector.tensor_copy if c == 0 and passes == UNIT else nc.scalar.copy
+                        copy(
+                            out=w_grouped[i][:, c, e].rearrange("p (g i) t -> p g t i", i=PACK),
+                            in_=w_raw[i, e][:, c].rearrange("p t (g i) -> p g t i", i=PACK),
                         )
 
-            slot = r % CODE_BUFS
+        def quantise_g(i):
+            if i >= count:
+                return
+            cols = units[i][2] * BATCH
+            slot = i % SLOTS
             nc.vector.quantize_mx(
-                out=g_codes[slot][:, :ROUND_COLS].bitcast(E5M2_X4),
-                scales=g_scales[slot][:, :ROUND_COLS],
-                in_=g_grouped[:],
+                out=g_codes[slot][:, :cols].bitcast(E5M2_X4),
+                scales=g_scales[slot][:, :cols],
+                in_=g_grouped[i][:],
             )
-            w_codes[r] = codes.tile([P, EDGES, ROUND_PASSES, IN_CH], U32, name="w_codes", align_bytes=64)
-            w_scales[r] = codes.tile([P, EDGES, ROUND_PASSES, IN_CH], U8, name="w_scales", align_bytes=64)
-            for e in range(len(edges)):
+
+        def quantise_w(i):
+            joint, pass0, passes = units[i]
+            cols = len(edges_of(joint)) * IN_CH
+            slot = i % SLOTS
+            for c in range(passes):
+                col0 = GAP + c * PASS_COLS
                 nc.vector.quantize_mx(
-                    out=w_codes[r][:, e].rearrange("p c i -> p (c i)").bitcast(E4M3_X4),
-                    scales=w_scales[r][:, e].rearrange("p c i -> p (c i)"),
-                    in_=w_grouped[:, e].rearrange("p c i t -> p (c i t)"),
+                    out=w_codes[slot][:, col0 : col0 + cols].bitcast(E4M3_X4),
+                    scales=w_scales[slot][:, col0 : col0 + cols],
+                    in_=w_grouped[i][:, c].rearrange("p e i t -> p (e i t)"),
                 )
 
-        def multiply(r):
-            joint, part = divmod(r, ROUNDS_PER_JOINT)
-            slot = r % CODE_BUFS
-            for e, (weight, target) in enumerate(edges_of(joint)):
-                opens = e == 0 and part == 0
-                closes = part == ROUNDS_PER_JOINT - 1 and (e == 1 or joint == JOINTS - 1)
-                for c in range(ROUND_PASSES):
+        def multiply(i):
+            joint, pass0, passes = units[i]
+            slot = i % SLOTS
+            for c in range(passes):
+                opens = pass0 + c == 0
+                closes = pass0 + c == PASSES - 1
+                col0 = GAP + c * PASS_COLS
+                if joint == 0:
+                    g0 = c * BATCH
                     nc.tensor.matmul_mx(
-                        out=acc[target][:],
-                        lhsT=w_codes[r][:, e, c, :].bitcast(E4M3_X4),
-                        lhsT_scale=w_scales[r][:, e, c, :],
-                        rhs=g_codes[slot][:, c * BATCH : c * BATCH + MOVING].bitcast(E5M2_X4),
-                        rhs_scale=g_scales[slot][:, c * BATCH : c * BATCH + MOVING],
-                        start=(opens and c == 0),
-                        stop=(closes and c == ROUND_PASSES - 1),
+                        out=acc_t[:],
+                        lhsT=w_codes[slot][:, col0 : col0 + IN_CH].bitcast(E4M3_X4),
+                        lhsT_scale=w_scales[slot][:, col0 : col0 + IN_CH],
+                        rhs=g_codes[slot][:, g0 : g0 + OUT_COLS].bitcast(E5M2_X4),
+                        rhs_scale=g_scales[slot][:, g0 : g0 + OUT_COLS],
+                        start=opens,
+                        stop=closes,
+                    )
+                    continue
+                w0 = col0 - (joint - 1) * IN_CH
+                for h in range(HALVES):
+                    g0 = c * BATCH + h * P
+                    nc.tensor.matmul_mx(
+                        out=acc[h][:],
+                        lhsT=g_codes[slot][:, g0 : g0 + P].bitcast(E5M2_X4),
+                        lhsT_scale=g_scales[slot][:, g0 : g0 + P],
+                        rhs=w_codes[slot][:, w0 : w0 + OUT_COLS].bitcast(E4M3_X4),
+                        rhs_scale=w_scales[slot][:, w0 : w0 + OUT_COLS],
+                        start=(joint == 1 and opens),
+                        stop=(joint == JOINTS - 1 and closes),
                     )
 
-        for r in range(ROUNDS + 1):
-            if r < ROUNDS:
-                prepare(r)
-            if r + RAW_BUFS < ROUNDS:
-                load(r + RAW_BUFS)
-            if r > 0:
-                multiply(r - 1)
+        transpose_g(0)
+        load_g(RAW_BUFS)
+        quantise_g(0)
+        for i in range(count):
+            transpose_g(i + 1)
+            load_g(i + 1 + RAW_BUFS)
+            group_w(i)
+            load_w(i + RAW_BUFS)
+            quantise_g(i + 1)
+            quantise_w(i)
+            if i > 0:
+                multiply(i - 1)
+            if i == PASSES // UNIT + 1:
+                nc.scalar.copy(out=sum_t[:], in_=acc_t[:, :BATCH])
+            if i == PASSES // UNIT + 2:
+                turned = banks.tile([P, HALVES, PAIR, P], F32, name="bank")
+                for h in range(HALVES):
+                    nc.tensor.transpose(turned[:, h, 0, :], sum_t[:, h * P : (h + 1) * P], identity[:])
+                nc.scalar.copy(out=first[:], in_=turned[:, :, 0, :])
+        multiply(count - 1)
 
-        copy_of = [nc.vector.tensor_copy if j % 2 == 0 else nc.scalar.copy for j in range(JOINTS)]
-        sum_t = [keep.tile([P, BATCH], F32, name="sum_t%d" % j) for j in range(JOINTS)]
-        out_sb = keep.tile([P, HALVES, JOINTS, IN_CH], F32, name="out_sb")
-        for j in range(JOINTS):
-            copy_of[j](out=sum_t[j][:], in_=acc[j][:, :BATCH])
-        turned = []
-        for j in range(JOINTS):
-            turned.append(banks.tile([P, HALVES, PAIR, P], F32, name="bank"))
-            for h in range(HALVES):
-                nc.tensor.transpose(turned[j][:, h, 0, :], sum_t[j][:, h * P : (h + 1) * P], identity[:])
-        for j in range(JOINTS):
-            copy_of[j](out=out_sb[:, :, j, :], in_=turned[j][:, :, 0, :])
-            nc.sync.dma_start(out=out_rows[:, :, j * IN_CH : (j + 1) * IN_CH], in_=out_sb[:, :, j, :])
+        out_sb = [keep.tile([P, OUT_COLS], F32, name="out_sb%d" % h) for h in range(HALVES)]
+        rest = slice(IN_CH, OUT_COLS)
+        copy_of = [nc.scalar.copy, nc.vector.tensor_copy]
+        for h in range(HALVES):
+            nc.vector.tensor_tensor(
+                out=out_sb[h][:, :IN_CH], in0=acc[h][:, :IN_CH], in1=first[:, h, :], op=mybir.AluOpType.add
+            )
+            copy_of[h](out=out_sb[h][:, rest], in_=acc[h][:, rest])
+            nc.sync.dma_start(out=out[h * P : (h + 1) * P, :], in_=out_sb[h][:])

@@ -26,6 +26,7 @@ OUT_COLS = JOINTS * IN_CH
 
 UNIT = 4
 LAST_UNITS = [4, 4, 4, 2, 1, 1]
+RUN = 2
 FIRST_PIECES = [1, 1, 2]
 
 EDGE_COLS = 2 * IN_CH
@@ -36,7 +37,8 @@ G_COLS = UNIT * BATCH
 PAD_COLS = OUT_COLS - BATCH
 
 RAW_BUFS = 5
-SLOTS = 4
+SLOTS = 5
+LAG = 2
 
 FLOPS = 2 * BATCH * OUT_CH * IN_CH * (2 * JOINTS - 1)
 
@@ -124,13 +126,17 @@ def tile_skeletonlinear_pa_k_kernel(tc, x, w_self, w_parent, bias, grad_out, out
         g_grouped = {}
         w_grouped = {}
 
-        def transpose_g(i):
+        def run(i, part):
+            passes = units[i][2]
+            return range(passes)[part * RUN : (part + 1) * RUN]
+
+        def transpose_g(i, part):
             if i >= count:
                 return
-            passes = units[i][2]
-            g_grouped[i] = grouped.tile([P, passes * BATCH * PACK], BF16, name="g_grouped", align_bytes=64)
+            if part == 0:
+                g_grouped[i] = grouped.tile([P, units[i][2] * BATCH * PACK], BF16, name="g_grouped", align_bytes=64)
             g_grouped_words = g_grouped[i][:].bitcast(F32)
-            for c in range(passes):
+            for c in run(i, part):
                 bank = banks.tile([P, HALVES, PAIR, P], F32, name="bank")
                 word0 = c * K_PASS // PAIR
                 for h in range(HALVES):
@@ -189,10 +195,12 @@ def tile_skeletonlinear_pa_k_kernel(tc, x, w_self, w_parent, bias, grad_out, out
                     in_=w_grouped[i][:, c].rearrange("p e i t -> p (e i t)"),
                 )
 
-        def multiply(i):
+        def multiply(i, part):
+            if i < 0:
+                return
             joint, pass0, passes = units[i]
             slot = i % SLOTS
-            for c in range(passes):
+            for c in run(i, part):
                 opens = pass0 + c == 0
                 closes = pass0 + c == PASSES - 1
                 col0 = GAP + c * PASS_COLS
@@ -221,26 +229,29 @@ def tile_skeletonlinear_pa_k_kernel(tc, x, w_self, w_parent, bias, grad_out, out
                         stop=(joint == JOINTS - 1 and closes),
                     )
 
-        transpose_g(0)
+        for part in range(UNIT // RUN):
+            transpose_g(0, part)
         load_g(RAW_BUFS)
         quantise_g(0)
         for i in range(count):
-            transpose_g(i + 1)
+            for part in range(UNIT // RUN):
+                transpose_g(i + 1, part)
+                multiply(i - LAG, part)
             load_g(i + 1 + RAW_BUFS)
             group_w(i)
             load_w(i + RAW_BUFS)
             quantise_g(i + 1)
             quantise_w(i)
-            if i > 0:
-                multiply(i - 1)
-            if i == PASSES // UNIT + 1:
+            if i == PASSES // UNIT + LAG:
                 nc.scalar.copy(out=sum_t[:], in_=acc_t[:, :BATCH])
-            if i == PASSES // UNIT + 2:
+            if i == PASSES // UNIT + LAG + 1:
                 turned = banks.tile([P, HALVES, PAIR, P], F32, name="bank")
                 for h in range(HALVES):
                     nc.tensor.transpose(turned[:, h, 0, :], sum_t[:, h * P : (h + 1) * P], identity[:])
                 nc.scalar.copy(out=first[:], in_=turned[:, :, 0, :])
-        multiply(count - 1)
+        for i in range(count - LAG, count):
+            for part in range(UNIT // RUN):
+                multiply(i, part)
 
         out_sb = [keep.tile([P, OUT_COLS], F32, name="out_sb%d" % h) for h in range(HALVES)]
         rest = slice(IN_CH, OUT_COLS)

@@ -22,23 +22,19 @@ JOINTS = 4
 IN_CH = 128
 OUT_CH = 8192
 PASSES = OUT_CH // K_PASS
-OUT_COLS = JOINTS * IN_CH
+MOVING = 512
 
 UNIT = 4
 LAST_UNITS = [4, 4, 4, 2, 1, 1]
-RUN = 2
 FIRST_PIECES = [1, 1, 2]
+RUN = 2
 
 EDGE_COLS = 2 * IN_CH
-GAP = OUT_COLS - EDGE_COLS
-PASS_COLS = EDGE_COLS + GAP
-W_COLS = UNIT * PASS_COLS + GAP
-G_COLS = UNIT * BATCH
-PAD_COLS = OUT_COLS - BATCH
+CODE_COLS = UNIT * 256
+PAD_COLS = MOVING - 256
 
 RAW_BUFS = 5
 SLOTS = 5
-LAG = 2
 
 FLOPS = 2 * BATCH * OUT_CH * IN_CH * (2 * JOINTS - 1)
 
@@ -46,6 +42,7 @@ FLOPS = 2 * BATCH * OUT_CH * IN_CH * (2 * JOINTS - 1)
 def tile_skeletonlinear_pa_k_kernel(tc, x, w_self, w_parent, bias, grad_out, out):
     nc = tc.nc
     g_rows = grad_out.rearrange("(h b) k -> b h k", h=HALVES)
+    out_rows = out.rearrange("(h b) c -> b h c", h=HALVES)
 
     def edges_of(joint):
         return [w_parent[joint - 1], w_self[joint]] if joint > 0 else [w_self[joint]]
@@ -64,7 +61,7 @@ def tile_skeletonlinear_pa_k_kernel(tc, x, w_self, w_parent, bias, grad_out, out
         raw = ctx.enter_context(tc.tile_pool(name="raw", bufs=RAW_BUFS))
         grouped = ctx.enter_context(tc.tile_pool(name="grouped", bufs=2))
         sums = ctx.enter_context(tc.psum_pool(name="sums", bufs=1))
-        banks = ctx.enter_context(tc.psum_pool(name="banks", bufs=5))
+        banks = ctx.enter_context(tc.psum_pool(name="banks", bufs=4))
 
         g_raw = {}
         w_raw = {}
@@ -96,7 +93,6 @@ def tile_skeletonlinear_pa_k_kernel(tc, x, w_self, w_parent, bias, grad_out, out
         for i in range(1, RAW_BUFS):
             load_g(i)
             load_w(i - 1)
-        load_w(RAW_BUFS - 1)
 
         identity = keep.tile([P, P], F32, name="identity")
         make_identity(nc, identity[:])
@@ -106,37 +102,31 @@ def tile_skeletonlinear_pa_k_kernel(tc, x, w_self, w_parent, bias, grad_out, out
         g_codes = []
         g_scales = []
         for i in range(SLOTS):
-            w_codes.append(keep.tile([P, W_COLS], U32, name="w_codes%d" % i, align_bytes=64))
-            w_scales.append(keep.tile([P, W_COLS], U8, name="w_scales%d" % i, align_bytes=64))
-            g_codes.append(keep.tile([P, G_COLS + PAD_COLS], U32, name="g_codes%d" % i, align_bytes=64))
-            g_scales.append(keep.tile([P, G_COLS + PAD_COLS], U8, name="g_scales%d" % i, align_bytes=64))
-            nc.gpsimd.memset(g_codes[i][:, G_COLS:].bitcast(I32), 0)
-            nc.gpsimd.memset(g_scales[i][:, G_COLS:].bitcast(I32), 0)
-            engine = nc.vector if i < SLOTS // 2 else nc.gpsimd
-            for plane in (w_codes[i][:], w_scales[i][:]):
-                words = plane.bitcast(I32)
-                blocks = words.rearrange("p (n w) -> p n w", n=W_COLS // GAP)
-                engine.memset(blocks[:, 0 : W_COLS // GAP : 2, :], 0)
+            for codes, scales, who in ((w_codes, w_scales, "w"), (g_codes, g_scales, "g")):
+                codes.append(keep.tile([P, CODE_COLS + PAD_COLS], U32, name="%s_codes%d" % (who, i), align_bytes=64))
+                scales.append(keep.tile([P, CODE_COLS + PAD_COLS], U8, name="%s_scales%d" % (who, i), align_bytes=64))
+                nc.gpsimd.memset(codes[i][:, CODE_COLS:].bitcast(I32), 0)
+                nc.gpsimd.memset(scales[i][:, CODE_COLS:].bitcast(I32), 0)
 
-        acc = [sums.tile([P, OUT_COLS], F32, name="acc%d" % h) for h in range(HALVES)]
-        acc_t = sums.tile([P, OUT_COLS], F32, name="acc_t")
+        acc = [[sums.tile([P, MOVING], F32, name="acc%d%d" % (j, h)) for h in range(HALVES)] for j in range(2)]
         sum_t = keep.tile([P, BATCH], F32, name="sum_t")
-        first = keep.tile([P, HALVES, IN_CH], F32, name="first")
+        part = [keep.tile([P, HALVES, EDGE_COLS], F32, name="part%d" % j) for j in range(JOINTS - 1)]
+        out_sb = [keep.tile([P, HALVES, IN_CH], F32, name="out_sb%d" % j) for j in range(JOINTS)]
 
         g_grouped = {}
         w_grouped = {}
 
-        def run(i, part):
-            passes = units[i][2]
-            return range(passes)[part * RUN : (part + 1) * RUN]
+        def inside(i):
+            return 0 <= i < count
 
-        def transpose_g(i, part):
-            if i >= count:
-                return
-            if part == 0:
+        def run(i, part):
+            return range(units[i][2])[part * RUN : (part + 1) * RUN]
+
+        def transpose_g(i, half):
+            if half == 0:
                 g_grouped[i] = grouped.tile([P, units[i][2] * BATCH * PACK], BF16, name="g_grouped", align_bytes=64)
             g_grouped_words = g_grouped[i][:].bitcast(F32)
-            for c in run(i, part):
+            for c in run(i, half):
                 bank = banks.tile([P, HALVES, PAIR, P], F32, name="bank")
                 word0 = c * K_PASS // PAIR
                 for h in range(HALVES):
@@ -166,15 +156,13 @@ def tile_skeletonlinear_pa_k_kernel(tc, x, w_self, w_parent, bias, grad_out, out
                     )
                 else:
                     for c in range(passes):
-                        copy = nc.vector.tensor_copy if c == 0 and passes == UNIT else nc.scalar.copy
+                        copy = nc.vector.tensor_copy if c == 0 and passes == UNIT and i % 2 == 0 else nc.scalar.copy
                         copy(
                             out=w_grouped[i][:, c, e].rearrange("p (g i) t -> p g t i", i=PACK),
                             in_=w_raw[i, e][:, c].rearrange("p t (g i) -> p g t i", i=PACK),
                         )
 
         def quantise_g(i):
-            if i >= count:
-                return
             cols = units[i][2] * BATCH
             slot = i % SLOTS
             nc.vector.quantize_mx(
@@ -185,80 +173,104 @@ def tile_skeletonlinear_pa_k_kernel(tc, x, w_self, w_parent, bias, grad_out, out
 
         def quantise_w(i):
             joint, pass0, passes = units[i]
-            cols = len(edges_of(joint)) * IN_CH
+            cols = passes * len(edges_of(joint)) * IN_CH
             slot = i % SLOTS
-            for c in range(passes):
-                col0 = GAP + c * PASS_COLS
-                nc.vector.quantize_mx(
-                    out=w_codes[slot][:, col0 : col0 + cols].bitcast(E4M3_X4),
-                    scales=w_scales[slot][:, col0 : col0 + cols],
-                    in_=w_grouped[i][:, c].rearrange("p e i t -> p (e i t)"),
-                )
+            nc.vector.quantize_mx(
+                out=w_codes[slot][:, :cols].bitcast(E4M3_X4),
+                scales=w_scales[slot][:, :cols],
+                in_=w_grouped[i][:].rearrange("p c e i t -> p (c e i t)"),
+            )
 
-        def multiply(i, part):
-            if i < 0:
-                return
+        def multiply(i, half):
             joint, pass0, passes = units[i]
             slot = i % SLOTS
-            for c in run(i, part):
+            pair = acc[1 - joint % 2]
+            for c in run(i, half):
                 opens = pass0 + c == 0
                 closes = pass0 + c == PASSES - 1
-                col0 = GAP + c * PASS_COLS
                 if joint == 0:
+                    w0 = c * IN_CH
                     g0 = c * BATCH
                     nc.tensor.matmul_mx(
-                        out=acc_t[:],
-                        lhsT=w_codes[slot][:, col0 : col0 + IN_CH].bitcast(E4M3_X4),
-                        lhsT_scale=w_scales[slot][:, col0 : col0 + IN_CH],
-                        rhs=g_codes[slot][:, g0 : g0 + OUT_COLS].bitcast(E5M2_X4),
-                        rhs_scale=g_scales[slot][:, g0 : g0 + OUT_COLS],
+                        out=pair[0][:],
+                        lhsT=w_codes[slot][:, w0 : w0 + IN_CH].bitcast(E4M3_X4),
+                        lhsT_scale=w_scales[slot][:, w0 : w0 + IN_CH],
+                        rhs=g_codes[slot][:, g0 : g0 + MOVING].bitcast(E5M2_X4),
+                        rhs_scale=g_scales[slot][:, g0 : g0 + MOVING],
                         start=opens,
                         stop=closes,
                     )
                     continue
-                w0 = col0 - (joint - 1) * IN_CH
+                w0 = c * EDGE_COLS
                 for h in range(HALVES):
                     g0 = c * BATCH + h * P
                     nc.tensor.matmul_mx(
-                        out=acc[h][:],
+                        out=pair[h][:],
                         lhsT=g_codes[slot][:, g0 : g0 + P].bitcast(E5M2_X4),
                         lhsT_scale=g_scales[slot][:, g0 : g0 + P],
-                        rhs=w_codes[slot][:, w0 : w0 + OUT_COLS].bitcast(E4M3_X4),
-                        rhs_scale=w_scales[slot][:, w0 : w0 + OUT_COLS],
-                        start=(joint == 1 and opens),
-                        stop=(joint == JOINTS - 1 and closes),
+                        rhs=w_codes[slot][:, w0 : w0 + MOVING].bitcast(E4M3_X4),
+                        rhs_scale=w_scales[slot][:, w0 : w0 + MOVING],
+                        start=opens,
+                        stop=closes,
                     )
 
-        for part in range(UNIT // RUN):
-            transpose_g(0, part)
-        load_g(RAW_BUFS)
-        quantise_g(0)
-        for i in range(count):
-            for part in range(UNIT // RUN):
-                transpose_g(i + 1, part)
-                multiply(i - LAG, part)
-            load_g(i + 1 + RAW_BUFS)
-            group_w(i)
-            load_w(i + RAW_BUFS)
-            quantise_g(i + 1)
-            quantise_w(i)
-            if i == PASSES // UNIT + LAG:
-                nc.scalar.copy(out=sum_t[:], in_=acc_t[:, :BATCH])
-            if i == PASSES // UNIT + LAG + 1:
-                turned = banks.tile([P, HALVES, PAIR, P], F32, name="bank")
-                for h in range(HALVES):
-                    nc.tensor.transpose(turned[:, h, 0, :], sum_t[:, h * P : (h + 1) * P], identity[:])
-                nc.scalar.copy(out=first[:], in_=turned[:, :, 0, :])
-        for i in range(count - LAG, count):
-            for part in range(UNIT // RUN):
-                multiply(i, part)
+        def take_out(joint):
+            pair = acc[1 - joint % 2]
+            if joint == 0:
+                nc.scalar.copy(out=sum_t[:], in_=pair[0][:, :BATCH])
+                return
+            for h in range(HALVES):
+                nc.scalar.copy(out=part[joint][:, h, :], in_=pair[h][:, :EDGE_COLS])
 
-        out_sb = [keep.tile([P, OUT_COLS], F32, name="out_sb%d" % h) for h in range(HALVES)]
-        rest = slice(IN_CH, OUT_COLS)
-        copy_of = [nc.scalar.copy, nc.vector.tensor_copy]
+        def turn_back():
+            bank = banks.tile([P, HALVES, PAIR, P], F32, name="bank")
+            for h in range(HALVES):
+                nc.tensor.transpose(bank[:, h, 0, :], sum_t[:, h * P : (h + 1) * P], identity[:])
+            nc.scalar.copy(out=part[0][:, :, IN_CH:], in_=bank[:, :, 0, :])
+
+        def store(joint):
+            nc.sync.dma_start(out=out_rows[:, :, joint * IN_CH : (joint + 1) * IN_CH], in_=out_sb[joint][:])
+
+        def finish(joint):
+            nc.gpsimd.tensor_tensor(
+                out=out_sb[joint][:],
+                in0=part[joint][:, :, IN_CH:],
+                in1=part[joint + 1][:, :, :IN_CH],
+                op=mybir.AluOpType.add,
+            )
+            store(joint)
+
+        for step in range(-1, count + 1):
+            for half in range(UNIT // RUN):
+                if inside(step + 1):
+                    transpose_g(step + 1, half)
+                if inside(step - 1):
+                    multiply(step - 1, half)
+            if inside(step + 1):
+                load_g(step + 1 + RAW_BUFS)
+            if inside(step):
+                quantise_w(step)
+            load_w(step + RAW_BUFS)
+            if inside(step + 1):
+                group_w(step + 1)
+                quantise_g(step + 1)
+            joint, unit = divmod(step - 2, PASSES // UNIT)
+            if 0 <= joint < JOINTS - 1:
+                if unit == PASSES // UNIT - 1:
+                    take_out(joint)
+                if unit == 0 and joint == 1:
+                    turn_back()
+            if step - 3 in (2 * (PASSES // UNIT), 3 * (PASSES // UNIT)):
+                finish((step - 3) // (PASSES // UNIT) - 2)
+
+        last = acc[1 - (JOINTS - 1) % 2]
         for h in range(HALVES):
             nc.vector.tensor_tensor(
-                out=out_sb[h][:, :IN_CH], in0=acc[h][:, :IN_CH], in1=first[:, h, :], op=mybir.AluOpType.add
+                out=out_sb[JOINTS - 2][:, h, :],
+                in0=last[h][:, :IN_CH],
+                in1=part[JOINTS - 2][:, h, IN_CH:],
+                op=mybir.AluOpType.add,
             )
-            copy_of[h](out=out_sb[h][:, rest], in_=acc[h][:, rest])
-            nc.sync.dma_start(out=out[h * P : (h + 1) * P, :], in_=out_sb[h][:])
+            nc.scalar.copy(out=out_sb[JOINTS - 1][:, h, :], in_=last[h][:, IN_CH:EDGE_COLS])
+        store(JOINTS - 2)
+        store(JOINTS - 1)

@@ -25,7 +25,7 @@ PASSES = OUT_CH // K_PASS
 MOVING = 512
 
 UNIT = 4
-LAST_UNITS = [4, 4, 4, 2, 1, 1]
+LAST_UNITS = [4, 4, 4, 2, 2]
 FIRST_PIECES = [1, 1, 2]
 RUN = 2
 
@@ -110,8 +110,10 @@ def tile_skeletonlinear_pa_k_kernel(tc, x, w_self, w_parent, bias, grad_out, out
 
         acc = [[sums.tile([P, MOVING], F32, name="acc%d%d" % (j, h)) for h in range(HALVES)] for j in range(2)]
         sum_t = keep.tile([P, BATCH], F32, name="sum_t")
-        part = [keep.tile([P, HALVES, EDGE_COLS], F32, name="part%d" % j) for j in range(JOINTS - 1)]
-        out_sb = [keep.tile([P, HALVES, IN_CH], F32, name="out_sb%d" % j) for j in range(JOINTS)]
+        part = [keep.tile([P, HALVES, EDGE_COLS + IN_CH], F32, name="part%d" % j) for j in range(JOINTS - 1)]
+        nc.gpsimd.memset(part[-1][:, :, EDGE_COLS:], 0.0)
+        out_sb = [keep.tile([P, HALVES, IN_CH], F32, name="out_sb%d" % j) for j in range(JOINTS - 2)]
+        out_last = [keep.tile([P, EDGE_COLS], F32, name="out_last%d" % h) for h in range(HALVES)]
 
         g_grouped = {}
         w_grouped = {}
@@ -185,10 +187,8 @@ def tile_skeletonlinear_pa_k_kernel(tc, x, w_self, w_parent, bias, grad_out, out
             joint, pass0, passes = units[i]
             slot = i % SLOTS
             pair = acc[1 - joint % 2]
-            for c in run(i, half):
-                opens = pass0 + c == 0
-                closes = pass0 + c == PASSES - 1
-                if joint == 0:
+            if joint == 0:
+                for c in run(i, half):
                     w0 = c * IN_CH
                     g0 = c * BATCH
                     nc.tensor.matmul_mx(
@@ -197,12 +197,13 @@ def tile_skeletonlinear_pa_k_kernel(tc, x, w_self, w_parent, bias, grad_out, out
                         lhsT_scale=w_scales[slot][:, w0 : w0 + IN_CH],
                         rhs=g_codes[slot][:, g0 : g0 + MOVING].bitcast(E5M2_X4),
                         rhs_scale=g_scales[slot][:, g0 : g0 + MOVING],
-                        start=opens,
-                        stop=closes,
+                        start=(pass0 + c == 0),
+                        stop=(pass0 + c == PASSES - 1),
                     )
-                    continue
-                w0 = c * EDGE_COLS
-                for h in range(HALVES):
+                return
+            for h in range(HALVES):
+                for c in run(i, half):
+                    w0 = c * EDGE_COLS
                     g0 = c * BATCH + h * P
                     nc.tensor.matmul_mx(
                         out=pair[h][:],
@@ -210,8 +211,8 @@ def tile_skeletonlinear_pa_k_kernel(tc, x, w_self, w_parent, bias, grad_out, out
                         lhsT_scale=g_scales[slot][:, g0 : g0 + P],
                         rhs=w_codes[slot][:, w0 : w0 + MOVING].bitcast(E4M3_X4),
                         rhs_scale=w_scales[slot][:, w0 : w0 + MOVING],
-                        start=opens,
-                        stop=closes,
+                        start=(pass0 + c == 0),
+                        stop=(pass0 + c == PASSES - 1),
                     )
 
         def take_out(joint):
@@ -220,25 +221,22 @@ def tile_skeletonlinear_pa_k_kernel(tc, x, w_self, w_parent, bias, grad_out, out
                 nc.scalar.copy(out=sum_t[:], in_=pair[0][:, :BATCH])
                 return
             for h in range(HALVES):
-                nc.scalar.copy(out=part[joint][:, h, :], in_=pair[h][:, :EDGE_COLS])
+                nc.scalar.copy(out=part[joint][:, h, :EDGE_COLS], in_=pair[h][:, :EDGE_COLS])
 
         def turn_back():
             bank = banks.tile([P, HALVES, PAIR, P], F32, name="bank")
             for h in range(HALVES):
                 nc.tensor.transpose(bank[:, h, 0, :], sum_t[:, h * P : (h + 1) * P], identity[:])
-            nc.scalar.copy(out=part[0][:, :, IN_CH:], in_=bank[:, :, 0, :])
-
-        def store(joint):
-            nc.sync.dma_start(out=out_rows[:, :, joint * IN_CH : (joint + 1) * IN_CH], in_=out_sb[joint][:])
+            nc.scalar.copy(out=part[0][:, :, IN_CH:EDGE_COLS], in_=bank[:, :, 0, :])
 
         def finish(joint):
             nc.gpsimd.tensor_tensor(
                 out=out_sb[joint][:],
-                in0=part[joint][:, :, IN_CH:],
+                in0=part[joint][:, :, IN_CH:EDGE_COLS],
                 in1=part[joint + 1][:, :, :IN_CH],
                 op=mybir.AluOpType.add,
             )
-            store(joint)
+            nc.sync.dma_start(out=out_rows[:, :, joint * IN_CH : (joint + 1) * IN_CH], in_=out_sb[joint][:])
 
         for step in range(-1, count + 1):
             for half in range(UNIT // RUN):
@@ -266,11 +264,9 @@ def tile_skeletonlinear_pa_k_kernel(tc, x, w_self, w_parent, bias, grad_out, out
         last = acc[1 - (JOINTS - 1) % 2]
         for h in range(HALVES):
             nc.vector.tensor_tensor(
-                out=out_sb[JOINTS - 2][:, h, :],
-                in0=last[h][:, :IN_CH],
-                in1=part[JOINTS - 2][:, h, IN_CH:],
+                out=out_last[h][:],
+                in0=last[h][:, :EDGE_COLS],
+                in1=part[-1][:, h, IN_CH:],
                 op=mybir.AluOpType.add,
             )
-            nc.scalar.copy(out=out_sb[JOINTS - 1][:, h, :], in_=last[h][:, IN_CH:EDGE_COLS])
-        store(JOINTS - 2)
-        store(JOINTS - 1)
+            nc.sync.dma_start(out=out[h * P : (h + 1) * P, (JOINTS - 2) * IN_CH :], in_=out_last[h][:])

@@ -27,6 +27,7 @@ MOVING = 512
 UNIT = 4
 LAST_UNITS = [4, 4, 4, 2, 2]
 FIRST_PIECES = [1, 1, 2]
+GROUP = 8
 RUN = 2
 
 EDGE_COLS = 2 * IN_CH
@@ -153,15 +154,15 @@ def tile_skeletonlinear_pa_k_kernel(tc, x, w_self, w_parent, bias, grad_out, out
             for e in range(edges):
                 if e == edges - 1:
                     nc.vector.tensor_copy(
-                        out=w_grouped[i][:, :, e].rearrange("p c (g i) t -> p c g t i", i=PACK),
-                        in_=w_raw[i, e][:].rearrange("p c t (g i) -> p c g t i", i=PACK),
+                        out=w_grouped[i][:, :, e].rearrange("p c (g i) t -> p c g t i", i=GROUP),
+                        in_=w_raw[i, e][:].rearrange("p c t (g i) -> p c g t i", i=GROUP),
                     )
                 else:
                     for c in range(passes):
                         copy = nc.vector.tensor_copy if c == 0 and passes == UNIT and i % 2 == 0 else nc.scalar.copy
                         copy(
-                            out=w_grouped[i][:, c, e].rearrange("p (g i) t -> p g t i", i=PACK),
-                            in_=w_raw[i, e][:, c].rearrange("p t (g i) -> p g t i", i=PACK),
+                            out=w_grouped[i][:, c, e].rearrange("p (g i) t -> p g t i", i=GROUP),
+                            in_=w_raw[i, e][:, c].rearrange("p t (g i) -> p g t i", i=GROUP),
                         )
 
         def quantise_g(i):

from contextlib import ExitStack

import concourse.mybir as mybir
from concourse.masks import make_identity

F32 = mybir.dt.float32
BF16 = mybir.dt.bfloat16
I32 = mybir.dt.int32
U32 = mybir.dt.uint32
U8 = mybir.dt.uint8
E4M3_X4 = mybir.dt.float8_e4m3fn_x4
E5M2_X4 = mybir.dt.float8_e5m2_x4

P = 128
PACK = 4
K_PASS = P * PACK
PAIR = 2

BATCH = 256
HALVES = BATCH // P
JOINTS = 4
IN_CH = 128
OUT_CH = 8192
PASSES = OUT_CH // K_PASS
MOVING = 512

UNIT = 4
LAST_UNITS = [4, 4, 4, 2, 2]
FIRST_PIECES = [1, 1, 2]
GROUP = 8
RUN = 2

EDGE_COLS = 2 * IN_CH
CODE_COLS = UNIT * 256
PAD_COLS = MOVING - 256

RAW_BUFS = 5
SLOTS = 5

FLOPS = 2 * BATCH * OUT_CH * IN_CH * (2 * JOINTS - 1)


def tile_skeletonlinear_pa_k_kernel(tc, x, w_self, w_parent, bias, grad_out, out):
    nc = tc.nc
    g_rows = grad_out.rearrange("(h b) k -> b h k", h=HALVES)
    out_rows = out.rearrange("(h b) c -> b h c", h=HALVES)

    def edges_of(joint):
        return [w_parent[joint - 1], w_self[joint]] if joint > 0 else [w_self[joint]]

    units = []
    for joint in range(JOINTS):
        pass0 = 0
        for passes in LAST_UNITS if joint == JOINTS - 1 else [UNIT] * (PASSES // UNIT):
            units.append((joint, pass0, passes))
            pass0 += passes
    count = len(units)

    with ExitStack() as ctx:
        ctx.enter_context(tc.manual_schedule())
        keep = ctx.enter_context(tc.tile_pool(name="keep", bufs=1))
        raw = ctx.enter_context(tc.tile_pool(name="raw", bufs=RAW_BUFS))
        grouped = ctx.enter_context(tc.tile_pool(name="grouped", bufs=2))
        sums = ctx.enter_context(tc.psum_pool(name="sums", bufs=1))
        banks = ctx.enter_context(tc.psum_pool(name="banks", bufs=4))

        g_raw = {}
        w_raw = {}

        def load_g(i):
            if i >= count:
                return
            joint, pass0, passes = units[i]
            col0 = joint * OUT_CH + pass0 * K_PASS
            g_raw[i] = raw.tile([P, HALVES, passes * K_PASS], BF16, name="g_raw")
            k0 = 0
            for n in FIRST_PIECES if i == 0 else [passes]:
                k1 = k0 + n * K_PASS
                nc.sync.dma_start(out=g_raw[i][:, :, k0:k1], in_=g_rows[:, :, col0 + k0 : col0 + k1])
                k0 = k1

        def load_w(i):
            if i >= count:
                return
            joint, pass0, passes = units[i]
            rows = slice(pass0 * K_PASS, (pass0 + passes) * K_PASS)
            for e, weight in enumerate(edges_of(joint)):
                w_raw[i, e] = raw.tile([P, passes, PACK, IN_CH], BF16, name="w_raw%d" % e)
                nc.sync.dma_start(
                    out=w_raw[i, e][:], in_=weight[rows, :].rearrange("(c p t) i -> p c t i", p=P, t=PACK)
                )

        load_g(0)
        for i in range(1, RAW_BUFS):
            load_g(i)
            load_w(i - 1)

        identity = keep.tile([P, P], F32, name="identity")
        make_identity(nc, identity[:])

        w_codes = []
        w_scales = []
        g_codes = []
        g_scales = []
        for i in range(SLOTS):
            for codes, scales, who in ((w_codes, w_scales, "w"), (g_codes, g_scales, "g")):
                codes.append(keep.tile([P, CODE_COLS + PAD_COLS], U32, name="%s_codes%d" % (who, i), align_bytes=64))
                scales.append(keep.tile([P, CODE_COLS + PAD_COLS], U8, name="%s_scales%d" % (who, i), align_bytes=64))
                nc.gpsimd.memset(codes[i][:, CODE_COLS:].bitcast(I32), 0)
                nc.gpsimd.memset(scales[i][:, CODE_COLS:].bitcast(I32), 0)

        acc = [[sums.tile([P, MOVING], F32, name="acc%d%d" % (j, h)) for h in range(HALVES)] for j in range(2)]
        sum_t = keep.tile([P, BATCH], F32, name="sum_t")
        part = [keep.tile([P, HALVES, EDGE_COLS + IN_CH], F32, name="part%d" % j) for j in range(JOINTS - 1)]
        nc.gpsimd.memset(part[-1][:, :, EDGE_COLS:], 0.0)
        out_sb = [keep.tile([P, HALVES, IN_CH], F32, name="out_sb%d" % j) for j in range(JOINTS - 2)]
        out_last = [keep.tile([P, EDGE_COLS], F32, name="out_last%d" % h) for h in range(HALVES)]

        g_grouped = {}
        w_grouped = {}

        def inside(i):
            return 0 <= i < count

        def run(i, part):
            return range(units[i][2])[part * RUN : (part + 1) * RUN]

        def transpose_g(i, half):
            if half == 0:
                g_grouped[i] = grouped.tile([P, units[i][2] * BATCH * PACK], BF16, name="g_grouped", align_bytes=64)
            g_grouped_words = g_grouped[i][:].bitcast(F32)
            for c in run(i, half):
                bank = banks.tile([P, HALVES, PAIR, P], F32, name="bank")
                word0 = c * K_PASS // PAIR
                for h in range(HALVES):
                    g_words = g_raw[i][:, h, :].bitcast(F32)
                    for u in range(PAIR):
                        nc.tensor.transpose(
                            bank[:, h, u, :],
                            g_words[:, word0 + u : word0 + K_PASS // PAIR : PAIR],
                            identity[:],
                        )
                nc.scalar.copy(
                    out=g_grouped_words[:, c * BATCH * PAIR : (c + 1) * BATCH * PAIR].rearrange(
                        "p (h b u) -> p h b u", h=HALVES, u=PAIR
                    ),
                    in_=bank[:].rearrange("p h u b -> p h b u"),
                )

        def group_w(i):
            joint, pass0, passes = units[i]
            edges = len(edges_of(joint))
            w_grouped[i] = grouped.tile([P, passes, edges, IN_CH, PACK], BF16, name="w_grouped", align_bytes=64)
            for e in range(edges):
                if e == edges - 1:
                    nc.vector.tensor_copy(
                        out=w_grouped[i][:, :, e].rearrange("p c (g i) t -> p c g t i", i=GROUP),
                        in_=w_raw[i, e][:].rearrange("p c t (g i) -> p c g t i", i=GROUP),
                    )
                else:
                    for c in range(passes):
                        copy = nc.vector.tensor_copy if c == 0 and passes == UNIT and i % 2 == 0 else nc.scalar.copy
                        copy(
                            out=w_grouped[i][:, c, e].rearrange("p (g i) t -> p g t i", i=GROUP),
                            in_=w_raw[i, e][:, c].rearrange("p t (g i) -> p g t i", i=GROUP),
                        )

        def quantise_g(i):
            cols = units[i][2] * BATCH
            slot = i % SLOTS
            nc.vector.quantize_mx(
                out=g_codes[slot][:, :cols].bitcast(E5M2_X4),
                scales=g_scales[slot][:, :cols],
                in_=g_grouped[i][:],
            )

        def quantise_w(i):
            joint, pass0, passes = units[i]
            cols = passes * len(edges_of(joint)) * IN_CH
            slot = i % SLOTS
            nc.vector.quantize_mx(
                out=w_codes[slot][:, :cols].bitcast(E4M3_X4),
                scales=w_scales[slot][:, :cols],
                in_=w_grouped[i][:].rearrange("p c e i t -> p (c e i t)"),
            )

        def multiply(i, half):
            joint, pass0, passes = units[i]
            slot = i % SLOTS
            pair = acc[1 - joint % 2]
            if joint == 0:
                for c in run(i, half):
                    w0 = c * IN_CH
                    g0 = c * BATCH
                    nc.tensor.matmul_mx(
                        out=pair[0][:],
                        lhsT=w_codes[slot][:, w0 : w0 + IN_CH].bitcast(E4M3_X4),
                        lhsT_scale=w_scales[slot][:, w0 : w0 + IN_CH],
                        rhs=g_codes[slot][:, g0 : g0 + MOVING].bitcast(E5M2_X4),
                        rhs_scale=g_scales[slot][:, g0 : g0 + MOVING],
                        start=(pass0 + c == 0),
                        stop=(pass0 + c == PASSES - 1),
                    )
                return
            for h in range(HALVES):
                for c in run(i, half):
                    w0 = c * EDGE_COLS
                    g0 = c * BATCH + h * P
                    nc.tensor.matmul_mx(
                        out=pair[h][:],
                        lhsT=g_codes[slot][:, g0 : g0 + P].bitcast(E5M2_X4),
                        lhsT_scale=g_scales[slot][:, g0 : g0 + P],
                        rhs=w_codes[slot][:, w0 : w0 + MOVING].bitcast(E4M3_X4),
                        rhs_scale=w_scales[slot][:, w0 : w0 + MOVING],
                        start=(pass0 + c == 0),
                        stop=(pass0 + c == PASSES - 1),
                    )

        def take_out(joint):
            pair = acc[1 - joint % 2]
            if joint == 0:
                nc.scalar.copy(out=sum_t[:], in_=pair[0][:, :BATCH])
                return
            for h in range(HALVES):
                nc.scalar.copy(out=part[joint][:, h, :EDGE_COLS], in_=pair[h][:, :EDGE_COLS])

        def turn_back():
            bank = banks.tile([P, HALVES, PAIR, P], F32, name="bank")
            for h in range(HALVES):
                nc.tensor.transpose(bank[:, h, 0, :], sum_t[:, h * P : (h + 1) * P], identity[:])
            nc.scalar.copy(out=part[0][:, :, IN_CH:EDGE_COLS], in_=bank[:, :, 0, :])

        def finish(joint):
            nc.gpsimd.tensor_tensor(
                out=out_sb[joint][:],
                in0=part[joint][:, :, IN_CH:EDGE_COLS],
                in1=part[joint + 1][:, :, :IN_CH],
                op=mybir.AluOpType.add,
            )
            nc.sync.dma_start(out=out_rows[:, :, joint * IN_CH : (joint + 1) * IN_CH], in_=out_sb[joint][:])

        for step in range(-1, count + 1):
            for half in range(UNIT // RUN):
                if inside(step + 1):
                    transpose_g(step + 1, half)
                if inside(step - 1):
                    multiply(step - 1, half)
            if inside(step + 1):
                load_g(step + 1 + RAW_BUFS)
            if inside(step):
                quantise_w(step)
            load_w(step + RAW_BUFS)
            if inside(step + 1):
                group_w(step + 1)
                quantise_g(step + 1)
            joint, unit = divmod(step - 2, PASSES // UNIT)
            if 0 <= joint < JOINTS - 1:
                if unit == PASSES // UNIT - 1:
                    take_out(joint)
                if unit == 0 and joint == 1:
                    turn_back()
            if step - 3 in (2 * (PASSES // UNIT), 3 * (PASSES // UNIT)):
                finish((step - 3) // (PASSES // UNIT) - 2)

        last = acc[1 - (JOINTS - 1) % 2]
        for h in range(HALVES):
            nc.vector.tensor_tensor(
                out=out_last[h][:],
                in0=last[h][:, :EDGE_COLS],
                in1=part[-1][:, h, IN_CH:],
                op=mybir.AluOpType.add,
            )
            nc.sync.dma_start(out=out[h * P : (h + 1) * P, (JOINTS - 2) * IN_CH :], in_=out_last[h][:])
